import numpy as np
import ml_dtypes


def mxq(x, axis, fmt="e4m3"):
    dtype, down = {"e4m3": (ml_dtypes.float8_e4m3fn, 7), "e5m2": (ml_dtypes.float8_e5m2, 14)}[fmt]
    v = np.moveaxis(np.asarray(x, np.float32).astype(ml_dtypes.bfloat16).astype(np.float64), axis, -1)
    blocks = v.reshape(v.shape[:-1] + (-1, 32))
    amax = np.abs(blocks).max(-1, keepdims=True)
    byte = np.maximum(np.where(amax > 0, np.frexp(amax)[1] - 1 + 127, 0) - down, 1)
    scale = np.exp2(byte - 127.0)
    codes = (blocks / scale).astype(np.float32).astype(dtype).astype(np.float64)
    return np.moveaxis((codes * scale).reshape(v.shape), -1, axis)


WIDE = False


def mx_kscale(k):
    if not WIDE:
        return np.ones(k)
    levels = np.array([10, -10, 5, -5, 0])
    a = np.random.permutation(np.resize(levels, k // 512 * 4)).reshape(k // 512, 4)
    idx = np.arange(k)
    return np.exp2(a[idx // 512, idx % 128 // 32])


BF16 = ml_dtypes.bfloat16


def bf(x):
    return np.asarray(x, np.float32).astype(BF16)


def f64(x):
    return np.asarray(x).astype(np.float64)


S, HID, NH, Q_LORA, KV_LORA, NOPE, ROPE, VDIM, BLK = 8192, 512, 4, 1536, 512, 64, 64, 64, 128
EPS = 1e-6


def blockscale(rows, cols, k, g):
    return bf((np.random.random((rows, cols)) * 0.8 + 0.2) * g / np.sqrt(k))


def dequant(w, s):
    so = np.repeat(s, BLK, axis=0)[: w.shape[0]]
    se = np.repeat(so, BLK, axis=1)[:, : w.shape[1]]
    return w * se


def rmsnorm(x, w):
    var = np.mean(x * x, axis=-1, keepdims=True)
    return x * (1.0 / np.sqrt(var + EPS)) * w


def setup_inputs():
    s, t = mx_kscale(HID), mx_kscale(KV_LORA)
    return {"hidden_states": bf(np.random.standard_normal((S, HID)) * s),
            "wkv_a_lat": bf(np.random.standard_normal((KV_LORA, HID)) / s[None, :]),
            "skv_a_lat": blockscale(KV_LORA // BLK, HID // BLK, HID, 1.0),
            "wkv_b": bf(np.random.standard_normal((NH * (NOPE + VDIM), KV_LORA)) / t[None, :]),
            "skv_b": blockscale(NH * (NOPE + VDIM) // BLK, KV_LORA // BLK, KV_LORA, 2.0),
            "kv_ln_w": bf((1.0 + 0.1 * np.random.standard_normal(KV_LORA)) * t)}


def reference(hidden_states, wkv_a_lat, skv_a_lat, wkv_b, skv_b, kv_ln_w):
    wa = dequant(f64(wkv_a_lat), f64(skv_a_lat))
    lkv = mxq(f64(hidden_states), 1, "e4m3") @ mxq(wa, 1, "e4m3").T
    kv_nope = rmsnorm(lkv, f64(kv_ln_w))
    wb = dequant(f64(wkv_b), f64(skv_b))
    kvb = (mxq(kv_nope, 1, "e4m3") @ mxq(wb, 1, "e4m3").T).reshape(S, NH, NOPE + VDIM)
    return kvb[..., :NOPE], kvb[..., NOPE:]

@@ -1,0 +1,263 @@
+from contextlib import ExitStack
+
+import concourse.mybir as mybir
+from concourse.masks import make_identity
+
+BF16 = mybir.dt.bfloat16
+F32 = mybir.dt.float32
+U32 = mybir.dt.uint32
+U8 = mybir.dt.uint8
+FP8X4 = mybir.dt.float8_e4m3fn_x4
+ACT = mybir.ActivationFunctionType
+ALU = mybir.AluOpType
+
+P = 128
+S = 8192
+K = 512
+N_OUT = 512
+BLK = 128
+HEADS = 4
+HALF = 64
+EPS = 1e-6
+
+WORDS = K // 2
+TILES = S // P
+PAIR = 2
+N_PAIRS = TILES // PAIR
+LOAD_TILES = 4
+STORE_TILES = 4
+
+FLOPS = 2 * 2 * S * K * N_OUT
+
+
+def tile_deepseekv3attention_pb_t_kernel(
+    tc, hidden_states, wkv_a_lat, skv_a_lat, wkv_b, skv_b, kv_ln_w, out_0, out_1
+):
+    nc = tc.nc
+
+    x_rows = hidden_states.rearrange("(p t) k -> p t k", t=TILES)
+    k_rows = out_0.rearrange("(p t) h d -> p t (h d)", t=TILES)
+    v_rows = out_1.rearrange("(p t) h d -> p t (h d)", t=TILES)
+
+    with ExitStack() as ctx:
+        keep = ctx.enter_context(tc.tile_pool(name="keep", bufs=1))
+        work = ctx.enter_context(tc.tile_pool(name="work", bufs=2))
+        stats = ctx.enter_context(tc.tile_pool(name="stats", bufs=3))
+        scratch = ctx.enter_context(tc.tile_pool(name="scratch", bufs=4))
+        results = ctx.enter_context(tc.tile_pool(name="results", bufs=3))
+        psum_words = ctx.enter_context(tc.psum_pool(name="psum_words", bufs=1))
+        psum_c = ctx.enter_context(tc.psum_pool(name="psum_c", bufs=2 * PAIR))
+        psum_kv = ctx.enter_context(tc.psum_pool(name="psum_kv", bufs=PAIR))
+        ctx.enter_context(tc.manual_schedule())
+
+        def load_weight(w, s, label):
+            raw = keep.tile([P, N_OUT // P, K], BF16, name="raw_" + label)
+            nc.sync.dma_start(out=raw[:], in_=w.rearrange("(b p) k -> p b k", p=P))
+            factors = keep.tile([P, (N_OUT // BLK) * (K // BLK)], BF16, name="factors_" + label)
+            nc.scalar.dma_start(
+                out=factors[:], in_=s.rearrange("a b -> (a b)").partition_broadcast(P)
+            )
+            return raw, factors
+
+        x_sb = []
+
+        def load_x(chunk):
+            x_chunk = keep.tile([P, LOAD_TILES, K], BF16, name="x%d" % chunk)
+            first = chunk * LOAD_TILES
+            nc.sync.dma_start(out=x_chunk[:], in_=x_rows[:, first : first + LOAD_TILES, :])
+            x_sb.append(x_chunk)
+
+        raw_a, factors_a = load_weight(wkv_a_lat, skv_a_lat, "a")
+        load_x(0)
+        raw_b, factors_b = load_weight(wkv_b, skv_b, "b")
+        gain = keep.tile([P, K], BF16, name="gain")
+        nc.scalar.dma_start(out=gain[:], in_=kv_ln_w.partition_broadcast(P))
+        for chunk in range(1, TILES // LOAD_TILES):
+            load_x(chunk)
+
+        ident = keep.tile([P, P], F32, name="ident")
+        make_identity(nc, ident[:])
+        eps = keep.tile([P, 1], F32, name="eps")
+        nc.vector.memset(eps[:], EPS)
+        warm = keep.tile([P, 1], F32, name="warm")
+        nc.scalar.activation(out=warm[:], in_=eps[:], func=ACT.Sqrt)
+
+        def to_partitions(rows, tag):
+            bank = psum_words.tile([P, PAIR, 2, P], F32, name=tag, tag=tag)
+            words = rows.bitcast(F32)
+            for j in range(PAIR):
+                for u in range(2):
+                    nc.tensor.transpose(
+                        bank[:, j, u, :], words[:, j, u * P : (u + 1) * P], ident[:]
+                    )
+            return bank
+
+        def regroup(copy, bank, grouped):
+            copy(
+                out=grouped.bitcast(F32).rearrange("p (j r u) -> p j r u", j=PAIR, u=2),
+                in_=bank[:].rearrange("p j u r -> p j r u"),
+            )
+
+        def prepare_weight(raw, factors, label):
+            blocks = (N_OUT // BLK) * (K // BLK)
+            scaled = keep.tile([P, N_OUT // P, K], BF16, name="scaled_" + label)
+            nc.vector.tensor_tensor(
+                out=scaled[:].rearrange("p b (i c) -> p (b i) c", c=BLK),
+                in0=raw[:].rearrange("p b (i c) -> p (b i) c", c=BLK),
+                in1=factors[:].unsqueeze(2).to_broadcast([P, blocks, BLK]),
+                op=ALU.mult,
+            )
+            grouped = keep.tile([P, N_OUT * 4], BF16, name="grouped_" + label, align_bytes=64)
+            width = PAIR * P * 4
+            for half, tag in enumerate(("x_words", "h_words")):
+                bank = to_partitions(scaled[:, half * PAIR : (half + 1) * PAIR, :], tag)
+                regroup(nc.vector.tensor_copy, bank, grouped[:, half * width : (half + 1) * width])
+            codes = keep.tile([P, N_OUT], U32, name="codes_" + label, align_bytes=64)
+            scales = keep.tile([P, N_OUT], U8, name="scales_" + label, align_bytes=64)
+            nc.vector.quantize_mx(out=codes[:].bitcast(FP8X4), scales=scales[:], in_=grouped[:])
+            return codes, scales
+
+        x_bank, x_grouped, x_codes, x_scales = {}, {}, {}, {}
+        c_bank, sum_sq, std, rstd = {}, {}, {}, {}
+        h_rows, h_bank, h_grouped, h_codes, h_scales = {}, {}, {}, {}, {}
+        kv_bank, kv_sb = {}, {}
+        weights = {}
+
+        def in_range(i):
+            return 0 <= i < N_PAIRS
+
+        def quantise(grouped, label):
+            codes = work.tile([P, PAIR * P], U32, name=label + "_codes", align_bytes=64)
+            scales = work.tile([P, PAIR * P], U8, name=label + "_scales", align_bytes=64)
+            nc.vector.quantize_mx(out=codes[:].bitcast(FP8X4), scales=scales[:], in_=grouped[:])
+            return codes, scales
+
+        def multiply(out, codes, scales, j, weight):
+            w_codes, w_scales = weights[weight]
+            cols = slice(j * P, (j + 1) * P)
+            nc.tensor.matmul_mx(
+                out=out[:],
+                lhsT=codes[:, cols].bitcast(FP8X4),
+                lhsT_scale=scales[:, cols],
+                rhs=w_codes[:].bitcast(FP8X4),
+                rhs_scale=w_scales[:],
+                start=True,
+                stop=True,
+            )
+
+        def transpose_x(i):
+            if in_range(i):
+                first = i * PAIR
+                x_chunk = x_sb[first // LOAD_TILES]
+                at = first % LOAD_TILES
+                x_bank[i] = to_partitions(x_chunk[:, at : at + PAIR, :], "x_words")
+
+        def regroup_x(i):
+            if in_range(i):
+                x_grouped[i] = work.tile([P, PAIR * P * 4], BF16, name="x_grouped", align_bytes=64)
+                copy = nc.vector.tensor_copy if i % 2 == 0 else nc.scalar.copy
+                regroup(copy, x_bank[i], x_grouped[i][:])
+
+        def quantise_x(i):
+            if in_range(i):
+                x_codes[i], x_scales[i] = quantise(x_grouped[i], "x")
+
+        def first_matmul(i):
+            if in_range(i):
+                c_bank[i] = []
+                for j in range(PAIR):
+                    c_ps = psum_c.tile([P, N_OUT], F32, name="c_ps")
+                    multiply(c_ps, x_codes[i], x_scales[i], j, "a")
+                    c_bank[i].append(c_ps)
+
+        def sum_squares(i):
+            if in_range(i):
+                sum_sq[i] = stats.tile([P, PAIR], F32, name="sum_sq")
+                for j in range(PAIR):
+                    squares = scratch.tile([P, N_OUT], BF16, name="squares")
+                    nc.scalar.activation(
+                        out=squares[:],
+                        in_=c_bank[i][j][:],
+                        func=ACT.Square,
+                        accum_out=sum_sq[i][:, j : j + 1],
+                    )
+
+        def root(i):
+            if in_range(i):
+                std[i] = stats.tile([P, PAIR], F32, name="std")
+                nc.scalar.activation(
+                    out=std[i][:], in_=sum_sq[i][:], func=ACT.Sqrt, bias=eps[:, 0:1], scale=1.0 / K
+                )
+
+        def normalise(i):
+            if in_range(i):
+                rstd[i] = stats.tile([P, PAIR], F32, name="rstd")
+                nc.vector.reciprocal(out=rstd[i][:], in_=std[i][:])
+                h_rows[i] = work.tile([P, PAIR, K], BF16, name="h_rows")
+                for j in range(PAIR):
+                    nc.vector.scalar_tensor_tensor(
+                        out=h_rows[i][:, j, :],
+                        in0=c_bank[i][j][:],
+                        scalar=rstd[i][:, j : j + 1],
+                        in1=gain[:],
+                        op0=ALU.mult,
+                        op1=ALU.mult,
+                    )
+
+        def transpose_h(i):
+            if in_range(i):
+                h_bank[i] = to_partitions(h_rows[i][:], "h_words")
+
+        def regroup_h(i):
+            if in_range(i):
+                h_grouped[i] = work.tile([P, PAIR * P * 4], BF16, name="h_grouped", align_bytes=64)
+                regroup(nc.vector.tensor_copy, h_bank[i], h_grouped[i][:])
+
+        def quantise_h(i):
+            if in_range(i):
+                h_codes[i], h_scales[i] = quantise(h_grouped[i], "h")
+
+        def second_matmul(i):
+            if in_range(i):
+                kv_bank[i] = []
+                for j in range(PAIR):
+                    kv_ps = psum_kv.tile([P, N_OUT], F32, name="kv_ps")
+                    multiply(kv_ps, h_codes[i], h_scales[i], j, "b")
+                    kv_bank[i].append(kv_ps)
+
+        def store(i):
+            if in_range(i):
+                first = i * PAIR
+                group = first // STORE_TILES
+                at = first % STORE_TILES
+                if at == 0:
+                    kv_sb[group] = results.tile([P, 2, STORE_TILES, HEADS * HALF], F32, name="kv_sb")
+                for j in range(PAIR):
+                    nc.scalar.copy(
+                        out=kv_sb[group][:, :, at + j, :].rearrange("p a (h d) -> p a h d", d=HALF),
+                        in_=kv_bank[i][j][:].rearrange("p (h a d) -> p a h d", a=2, d=HALF),
+                    )
+                if at + PAIR == STORE_TILES:
+                    tiles = slice(group * STORE_TILES, (group + 1) * STORE_TILES)
+                    nc.sync.dma_start(out=k_rows[:, tiles, :], in_=kv_sb[group][:, 0, :, :])
+                    nc.sync.dma_start(out=v_rows[:, tiles, :], in_=kv_sb[group][:, 1, :, :])
+
+        def step(n):
+            transpose_x(n + 3)
+            regroup_h(n - 1)
+            quantise_x(n + 2)
+            normalise(n)
+            transpose_h(n)
+            quantise_h(n - 1)
+            regroup_x(n + 3)
+            first_matmul(n + 2)
+            second_matmul(n - 1)
+            sum_squares(n + 2)
+            store(n - 1)
+            root(n + 2)
+
+        weights["a"] = prepare_weight(raw_a, factors_a, "a")
+        step(-3)
+        weights["b"] = prepare_weight(raw_b, factors_b, "b")
+        for n in range(-2, N_PAIRS + 1):
+            step(n)

@@ -25,7 +25,6 @@ TILES = S // P
 PAIR = 2
 N_PAIRS = TILES // PAIR
 LOAD_TILES = 4
-STORE_TILES = 4
 
 FLOPS = 2 * 2 * S * K * N_OUT
 
@@ -42,13 +41,13 @@ def tile_deepseekv3attention_pb_t_kernel(
     with ExitStack() as ctx:
         keep = ctx.enter_context(tc.tile_pool(name="keep", bufs=1))
         work = ctx.enter_context(tc.tile_pool(name="work", bufs=2))
+        ahead = ctx.enter_context(tc.tile_pool(name="ahead", bufs=8))
         stats = ctx.enter_context(tc.tile_pool(name="stats", bufs=3))
         scratch = ctx.enter_context(tc.tile_pool(name="scratch", bufs=4))
-        results = ctx.enter_context(tc.tile_pool(name="results", bufs=3))
-        psum_words = ctx.enter_context(tc.psum_pool(name="psum_words", bufs=1))
+        results = ctx.enter_context(tc.tile_pool(name="results", bufs=4))
+        psum_words = ctx.enter_context(tc.psum_pool(name="psum_words", bufs=2))
         psum_c = ctx.enter_context(tc.psum_pool(name="psum_c", bufs=2 * PAIR))
         psum_kv = ctx.enter_context(tc.psum_pool(name="psum_kv", bufs=PAIR))
-        ctx.enter_context(tc.manual_schedule())
 
         def load_weight(w, s, label):
             raw = keep.tile([P, N_OUT // P, K], BF16, name="raw_" + label)
@@ -82,8 +81,8 @@ def tile_deepseekv3attention_pb_t_kernel(
         warm = keep.tile([P, 1], F32, name="warm")
         nc.scalar.activation(out=warm[:], in_=eps[:], func=ACT.Sqrt)
 
-        def to_partitions(rows, tag):
-            bank = psum_words.tile([P, PAIR, 2, P], F32, name=tag, tag=tag)
+        def to_partitions(rows, pool, name):
+            bank = pool.tile([P, PAIR, 2, P], F32, name=name)
             words = rows.bitcast(F32)
             for j in range(PAIR):
                 for u in range(2):
@@ -98,7 +97,7 @@ def tile_deepseekv3attention_pb_t_kernel(
                 in_=bank[:].rearrange("p j u r -> p j r u"),
             )
 
-        def prepare_weight(raw, factors, label):
+        def scale_weight(raw, factors, label):
             blocks = (N_OUT // BLK) * (K // BLK)
             scaled = keep.tile([P, N_OUT // P, K], BF16, name="scaled_" + label)
             nc.vector.tensor_tensor(
@@ -107,11 +106,17 @@ def tile_deepseekv3attention_pb_t_kernel(
                 in1=factors[:].unsqueeze(2).to_broadcast([P, blocks, BLK]),
                 op=ALU.mult,
             )
+            return scaled
+
+        def regroup_weight(copy, scaled, label):
             grouped = keep.tile([P, N_OUT * 4], BF16, name="grouped_" + label, align_bytes=64)
             width = PAIR * P * 4
-            for half, tag in enumerate(("x_words", "h_words")):
-                bank = to_partitions(scaled[:, half * PAIR : (half + 1) * PAIR, :], tag)
-                regroup(nc.vector.tensor_copy, bank, grouped[:, half * width : (half + 1) * width])
+            for half in range(N_OUT // P // PAIR):
+                bank = to_partitions(scaled[:, half * PAIR : (half + 1) * PAIR, :], psum_kv, "kv_ps")
+                regroup(copy, bank, grouped[:, half * width : (half + 1) * width])
+            return grouped
+
+        def quantise_weight(grouped, label):
             codes = keep.tile([P, N_OUT], U32, name="codes_" + label, align_bytes=64)
             scales = keep.tile([P, N_OUT], U8, name="scales_" + label, align_bytes=64)
             nc.vector.quantize_mx(out=codes[:].bitcast(FP8X4), scales=scales[:], in_=grouped[:])
@@ -120,15 +125,15 @@ def tile_deepseekv3attention_pb_t_kernel(
         x_bank, x_grouped, x_codes, x_scales = {}, {}, {}, {}
         c_bank, sum_sq, std, rstd = {}, {}, {}, {}
         h_rows, h_bank, h_grouped, h_codes, h_scales = {}, {}, {}, {}, {}
-        kv_bank, kv_sb = {}, {}
+        kv_bank = {}
         weights = {}
 
         def in_range(i):
             return 0 <= i < N_PAIRS
 
-        def quantise(grouped, label):
-            codes = work.tile([P, PAIR * P], U32, name=label + "_codes", align_bytes=64)
-            scales = work.tile([P, PAIR * P], U8, name=label + "_scales", align_bytes=64)
+        def quantise(pool, grouped, label):
+            codes = pool.tile([P, PAIR * P], U32, name=label + "_codes", align_bytes=64)
+            scales = pool.tile([P, PAIR * P], U8, name=label + "_scales", align_bytes=64)
             nc.vector.quantize_mx(out=codes[:].bitcast(FP8X4), scales=scales[:], in_=grouped[:])
             return codes, scales
 
@@ -150,17 +155,17 @@ def tile_deepseekv3attention_pb_t_kernel(
                 first = i * PAIR
                 x_chunk = x_sb[first // LOAD_TILES]
                 at = first % LOAD_TILES
-                x_bank[i] = to_partitions(x_chunk[:, at : at + PAIR, :], "x_words")
+                x_bank[i] = to_partitions(x_chunk[:, at : at + PAIR, :], psum_words, "words")
 
         def regroup_x(i):
             if in_range(i):
                 x_grouped[i] = work.tile([P, PAIR * P * 4], BF16, name="x_grouped", align_bytes=64)
-                copy = nc.vector.tensor_copy if i % 2 == 0 else nc.scalar.copy
+                copy = nc.vector.tensor_copy if i % 3 == 2 else nc.scalar.copy
                 regroup(copy, x_bank[i], x_grouped[i][:])
 
         def quantise_x(i):
             if in_range(i):
-                x_codes[i], x_scales[i] = quantise(x_grouped[i], "x")
+                x_codes[i], x_scales[i] = quantise(ahead, x_grouped[i], "x")
 
         def first_matmul(i):
             if in_range(i):
@@ -206,7 +211,7 @@ def tile_deepseekv3attention_pb_t_kernel(
 
         def transpose_h(i):
             if in_range(i):
-                h_bank[i] = to_partitions(h_rows[i][:], "h_words")
+                h_bank[i] = to_partitions(h_rows[i][:], psum_words, "words")
 
         def regroup_h(i):
             if in_range(i):
@@ -215,7 +220,7 @@ def tile_deepseekv3attention_pb_t_kernel(
 
         def quantise_h(i):
             if in_range(i):
-                h_codes[i], h_scales[i] = quantise(h_grouped[i], "h")
+                h_codes[i], h_scales[i] = quantise(work, h_grouped[i], "h")
 
         def second_matmul(i):
             if in_range(i):
@@ -227,37 +232,38 @@ def tile_deepseekv3attention_pb_t_kernel(
 
         def store(i):
             if in_range(i):
-                first = i * PAIR
-                group = first // STORE_TILES
-                at = first % STORE_TILES
-                if at == 0:
-                    kv_sb[group] = results.tile([P, 2, STORE_TILES, HEADS * HALF], F32, name="kv_sb")
+                kv_sb = results.tile([P, 2, PAIR, HEADS * HALF], F32, name="kv_sb")
                 for j in range(PAIR):
                     nc.scalar.copy(
-                        out=kv_sb[group][:, :, at + j, :].rearrange("p a (h d) -> p a h d", d=HALF),
+                        out=kv_sb[:, :, j, :].rearrange("p a (h d) -> p a h d", d=HALF),
                         in_=kv_bank[i][j][:].rearrange("p (h a d) -> p a h d", a=2, d=HALF),
                     )
-                if at + PAIR == STORE_TILES:
-                    tiles = slice(group * STORE_TILES, (group + 1) * STORE_TILES)
-                    nc.sync.dma_start(out=k_rows[:, tiles, :], in_=kv_sb[group][:, 0, :, :])
-                    nc.sync.dma_start(out=v_rows[:, tiles, :], in_=kv_sb[group][:, 1, :, :])
+                tiles = slice(i * PAIR, (i + 1) * PAIR)
+                nc.sync.dma_start(out=k_rows[:, tiles, :], in_=kv_sb[:, 0, :, :])
+                nc.sync.dma_start(out=v_rows[:, tiles, :], in_=kv_sb[:, 1, :, :])
 
         def step(n):
-            transpose_x(n + 3)
-            regroup_h(n - 1)
+            quantise_h(n - 2)
             quantise_x(n + 2)
+            second_matmul(n - 2)
             normalise(n)
-            transpose_h(n)
-            quantise_h(n - 1)
-            regroup_x(n + 3)
             first_matmul(n + 2)
-            second_matmul(n - 1)
+            regroup_h(n - 1)
+            transpose_h(n)
+            regroup_x(n + 3)
+            transpose_x(n + 4)
+            store(n - 2)
             sum_squares(n + 2)
-            store(n - 1)
             root(n + 2)
 
-        weights["a"] = prepare_weight(raw_a, factors_a, "a")
+        scaled_a = scale_weight(raw_a, factors_a, "a")
+        scaled_b = scale_weight(raw_b, factors_b, "b")
+        step(-4)
         step(-3)
-        weights["b"] = prepare_weight(raw_b, factors_b, "b")
-        for n in range(-2, N_PAIRS + 1):
+        grouped_a = regroup_weight(nc.vector.tensor_copy, scaled_a, "a")
+        weights["a"] = quantise_weight(grouped_a, "a")
+        grouped_b = regroup_weight(nc.scalar.copy, scaled_b, "b")
+        step(-2)
+        weights["b"] = quantise_weight(grouped_b, "b")
+        for n in range(-1, N_PAIRS + 2):
             step(n)

@@ -48,6 +48,7 @@ def tile_deepseekv3attention_pb_t_kernel(
         psum_words = ctx.enter_context(tc.psum_pool(name="psum_words", bufs=2))
         psum_c = ctx.enter_context(tc.psum_pool(name="psum_c", bufs=2 * PAIR))
         psum_kv = ctx.enter_context(tc.psum_pool(name="psum_kv", bufs=PAIR))
+        ctx.enter_context(tc.manual_schedule())
 
         def load_weight(w, s, label):
             raw = keep.tile([P, N_OUT // P, K], BF16, name="raw_" + label)
@@ -79,7 +80,7 @@ def tile_deepseekv3attention_pb_t_kernel(
         eps = keep.tile([P, 1], F32, name="eps")
         nc.vector.memset(eps[:], EPS)
         warm = keep.tile([P, 1], F32, name="warm")
-        nc.scalar.activation(out=warm[:], in_=eps[:], func=ACT.Sqrt)
+        nc.scalar.activation(out=warm[:], in_=eps[:], func=ACT.Abs_reciprocal_sqrt)
 
         def to_partitions(rows, pool, name):
             bank = pool.tile([P, PAIR, 2, P], F32, name=name)
@@ -123,9 +124,9 @@ def tile_deepseekv3attention_pb_t_kernel(
             return codes, scales
 
         x_bank, x_grouped, x_codes, x_scales = {}, {}, {}, {}
-        c_bank, sum_sq, std, rstd = {}, {}, {}, {}
+        c_bank, sum_sq, rstd = {}, {}, {}
         h_rows, h_bank, h_grouped, h_codes, h_scales = {}, {}, {}, {}, {}
-        kv_bank = {}
+        kv_bank, kv_sb = {}, {}
         weights = {}
 
         def in_range(i):
@@ -159,7 +160,7 @@ def tile_deepseekv3attention_pb_t_kernel(
 
         def regroup_x(i):
             if in_range(i):
-                x_grouped[i] = work.tile([P, PAIR * P * 4], BF16, name="x_grouped", align_bytes=64)
+                x_grouped[i] = scratch.tile([P, PAIR * P * 4], BF16, name="x_grouped", align_bytes=64)
                 copy = nc.vector.tensor_copy if i % 3 == 2 else nc.scalar.copy
                 regroup(copy, x_bank[i], x_grouped[i][:])
 
@@ -189,15 +190,17 @@ def tile_deepseekv3attention_pb_t_kernel(
 
         def root(i):
             if in_range(i):
-                std[i] = stats.tile([P, PAIR], F32, name="std")
+                rstd[i] = stats.tile([P, PAIR], F32, name="rstd")
                 nc.scalar.activation(
-                    out=std[i][:], in_=sum_sq[i][:], func=ACT.Sqrt, bias=eps[:, 0:1], scale=1.0 / K
+                    out=rstd[i][:],
+                    in_=sum_sq[i][:],
+                    func=ACT.Abs_reciprocal_sqrt,
+                    bias=eps[:, 0:1],
+                    scale=1.0 / K,
                 )
 
         def normalise(i):
             if in_range(i):
-                rstd[i] = stats.tile([P, PAIR], F32, name="rstd")
-                nc.vector.reciprocal(out=rstd[i][:], in_=std[i][:])
                 h_rows[i] = work.tile([P, PAIR, K], BF16, name="h_rows")
                 for j in range(PAIR):
                     nc.vector.scalar_tensor_tensor(
@@ -230,39 +233,45 @@ def tile_deepseekv3attention_pb_t_kernel(
                     multiply(kv_ps, h_codes[i], h_scales[i], j, "b")
                     kv_bank[i].append(kv_ps)
 
+        def copy_out(i, j):
+            if in_range(i):
+                if j == 0:
+                    kv_sb[i] = results.tile([P, 2, PAIR, HEADS * HALF], F32, name="kv_sb")
+                nc.scalar.copy(
+                    out=kv_sb[i][:, :, j, :].rearrange("p a (h d) -> p a h d", d=HALF),
+                    in_=kv_bank[i][j][:].rearrange("p (h a d) -> p a h d", a=2, d=HALF),
+                )
+
         def store(i):
             if in_range(i):
-                kv_sb = results.tile([P, 2, PAIR, HEADS * HALF], F32, name="kv_sb")
-                for j in range(PAIR):
-                    nc.scalar.copy(
-                        out=kv_sb[:, :, j, :].rearrange("p a (h d) -> p a h d", d=HALF),
-                        in_=kv_bank[i][j][:].rearrange("p (h a d) -> p a h d", a=2, d=HALF),
-                    )
                 tiles = slice(i * PAIR, (i + 1) * PAIR)
-                nc.sync.dma_start(out=k_rows[:, tiles, :], in_=kv_sb[:, 0, :, :])
-                nc.sync.dma_start(out=v_rows[:, tiles, :], in_=kv_sb[:, 1, :, :])
+                nc.sync.dma_start(out=k_rows[:, tiles, :], in_=kv_sb[i][:, 0, :, :])
+                nc.sync.dma_start(out=v_rows[:, tiles, :], in_=kv_sb[i][:, 1, :, :])
 
         def step(n):
-            quantise_h(n - 2)
             quantise_x(n + 2)
-            second_matmul(n - 2)
             normalise(n)
             first_matmul(n + 2)
+            quantise_h(n - 2)
+            second_matmul(n - 2)
             regroup_h(n - 1)
             transpose_h(n)
-            regroup_x(n + 3)
-            transpose_x(n + 4)
-            store(n - 2)
+            regroup_x(n + 4)
+            transpose_x(n + 5)
             sum_squares(n + 2)
+            copy_out(n - 2, 0)
             root(n + 2)
+            copy_out(n - 2, 1)
+            store(n - 2)
 
         scaled_a = scale_weight(raw_a, factors_a, "a")
         scaled_b = scale_weight(raw_b, factors_b, "b")
+        step(-5)
         step(-4)
-        step(-3)
         grouped_a = regroup_weight(nc.vector.tensor_copy, scaled_a, "a")
         weights["a"] = quantise_weight(grouped_a, "a")
         grouped_b = regroup_weight(nc.scalar.copy, scaled_b, "b")
+        step(-3)
         step(-2)
         weights["b"] = quantise_weight(grouped_b, "b")
         for n in range(-1, N_PAIRS + 2):

@@ -161,7 +161,7 @@ def tile_deepseekv3attention_pb_t_kernel(
         def regroup_x(i):
             if in_range(i):
                 x_grouped[i] = scratch.tile([P, PAIR * P * 4], BF16, name="x_grouped", align_bytes=64)
-                copy = nc.vector.tensor_copy if i % 3 == 2 else nc.scalar.copy
+                copy = nc.vector.tensor_copy if i % 2 == 1 else nc.scalar.copy
                 regroup(copy, x_bank[i], x_grouped[i][:])
 
         def quantise_x(i):

@@ -44,36 +44,62 @@ def tile_deepseekv3attention_pb_t_kernel(
         ahead = ctx.enter_context(tc.tile_pool(name="ahead", bufs=8))
         stats = ctx.enter_context(tc.tile_pool(name="stats", bufs=3))
         scratch = ctx.enter_context(tc.tile_pool(name="scratch", bufs=4))
-        results = ctx.enter_context(tc.tile_pool(name="results", bufs=4))
+        results = ctx.enter_context(tc.tile_pool(name="results", bufs=8))
         psum_words = ctx.enter_context(tc.psum_pool(name="psum_words", bufs=2))
         psum_c = ctx.enter_context(tc.psum_pool(name="psum_c", bufs=2 * PAIR))
         psum_kv = ctx.enter_context(tc.psum_pool(name="psum_kv", bufs=PAIR))
         ctx.enter_context(tc.manual_schedule())
 
-        def load_weight(w, s, label):
-            raw = keep.tile([P, N_OUT // P, K], BF16, name="raw_" + label)
-            nc.sync.dma_start(out=raw[:], in_=w.rearrange("(b p) k -> p b k", p=P))
+        HALVES = N_OUT // P // PAIR
+
+        def new_raw(label):
+            return keep.tile([P, N_OUT // P, K], BF16, name="raw_" + label)
+
+        def load_weight(raw, w, half):
+            rows = w.rearrange("(b p) k -> p b k", p=P)
+            blocks = slice(half * PAIR, (half + 1) * PAIR)
+            nc.sync.dma_start(out=raw[:, blocks, :], in_=rows[:, blocks, :])
+
+        def load_factors(s, label):
             factors = keep.tile([P, (N_OUT // BLK) * (K // BLK)], BF16, name="factors_" + label)
             nc.scalar.dma_start(
                 out=factors[:], in_=s.rearrange("a b -> (a b)").partition_broadcast(P)
             )
-            return raw, factors
+            return factors
 
         x_sb = []
 
-        def load_x(chunk):
+        def load_x(chunk, pieces):
             x_chunk = keep.tile([P, LOAD_TILES, K], BF16, name="x%d" % chunk)
-            first = chunk * LOAD_TILES
-            nc.sync.dma_start(out=x_chunk[:], in_=x_rows[:, first : first + LOAD_TILES, :])
             x_sb.append(x_chunk)
+            for piece in range(pieces):
+                load_piece(chunk, pieces, piece)
 
-        raw_a, factors_a = load_weight(wkv_a_lat, skv_a_lat, "a")
-        load_x(0)
-        raw_b, factors_b = load_weight(wkv_b, skv_b, "b")
+        def new_x(chunk):
+            x_sb.append(keep.tile([P, LOAD_TILES, K], BF16, name="x%d" % chunk))
+
+        def load_piece(chunk, pieces, piece):
+            width = LOAD_TILES // pieces
+            at = piece * width
+            first = chunk * LOAD_TILES + at
+            nc.sync.dma_start(
+                out=x_sb[chunk][:, at : at + width, :], in_=x_rows[:, first : first + width, :]
+            )
+
+        factors_a = load_factors(skv_a_lat, "a")
+        raw_a = new_raw("a")
+        raw_b = new_raw("b")
+        load_weight(raw_a, wkv_a_lat, 0)
+        load_weight(raw_a, wkv_a_lat, 1)
+        load_x(0, 2)
+        factors_b = load_factors(skv_b, "b")
+        load_weight(raw_b, wkv_b, 0)
+        load_weight(raw_b, wkv_b, 1)
         gain = keep.tile([P, K], BF16, name="gain")
         nc.scalar.dma_start(out=gain[:], in_=kv_ln_w.partition_broadcast(P))
-        for chunk in range(1, TILES // LOAD_TILES):
-            load_x(chunk)
+        load_x(1, 2)
+        for chunk in range(2, TILES // LOAD_TILES):
+            load_x(chunk, 1)
 
         ident = keep.tile([P, P], F32, name="ident")
         make_identity(nc, ident[:])
@@ -98,36 +124,58 @@ def tile_deepseekv3attention_pb_t_kernel(
                 in_=bank[:].rearrange("p j u r -> p j r u"),
             )
 
-        def scale_weight(raw, factors, label):
-            blocks = (N_OUT // BLK) * (K // BLK)
-            scaled = keep.tile([P, N_OUT // P, K], BF16, name="scaled_" + label)
-            nc.vector.tensor_tensor(
-                out=scaled[:].rearrange("p b (i c) -> p (b i) c", c=BLK),
-                in0=raw[:].rearrange("p b (i c) -> p (b i) c", c=BLK),
-                in1=factors[:].unsqueeze(2).to_broadcast([P, blocks, BLK]),
-                op=ALU.mult,
-            )
-            return scaled
+        WIDTH = PAIR * P * 4
+        weight = {}
+        weights = {}
 
-        def regroup_weight(copy, scaled, label):
-            grouped = keep.tile([P, N_OUT * 4], BF16, name="grouped_" + label, align_bytes=64)
-            width = PAIR * P * 4
-            for half in range(N_OUT // P // PAIR):
-                bank = to_partitions(scaled[:, half * PAIR : (half + 1) * PAIR, :], psum_kv, "kv_ps")
-                regroup(copy, bank, grouped[:, half * width : (half + 1) * width])
-            return grouped
-
-        def quantise_weight(grouped, label):
+        def new_weight(label, raw, factors):
+            weight[label] = {
+                "raw": raw,
+                "factors": factors,
+                "scaled": keep.tile([P, N_OUT // P, K], BF16, name="scaled_" + label),
+                "grouped": keep.tile([P, N_OUT * 4], BF16, name="grouped_" + label, align_bytes=64),
+                "bank": {},
+            }
             codes = keep.tile([P, N_OUT], U32, name="codes_" + label, align_bytes=64)
             scales = keep.tile([P, N_OUT], U8, name="scales_" + label, align_bytes=64)
-            nc.vector.quantize_mx(out=codes[:].bitcast(FP8X4), scales=scales[:], in_=grouped[:])
-            return codes, scales
+            weights[label] = (codes, scales)
+
+        def scale_weight(label, half):
+            w = weight[label]
+            blocks = PAIR * (K // BLK)
+            rows = slice(half * PAIR, (half + 1) * PAIR)
+            nc.vector.tensor_tensor(
+                out=w["scaled"][:, rows, :].rearrange("p b (i c) -> p (b i) c", c=BLK),
+                in0=w["raw"][:, rows, :].rearrange("p b (i c) -> p (b i) c", c=BLK),
+                in1=w["factors"][:, half * blocks : (half + 1) * blocks]
+                .unsqueeze(2)
+                .to_broadcast([P, blocks, BLK]),
+                op=ALU.mult,
+            )
+
+        def transpose_weight(label, half):
+            w = weight[label]
+            w["bank"][half] = to_partitions(
+                w["scaled"][:, half * PAIR : (half + 1) * PAIR, :], psum_kv, "kv_ps"
+            )
+
+        def regroup_weight(copy, label, half):
+            w = weight[label]
+            regroup(copy, w["bank"][half], w["grouped"][:, half * WIDTH : (half + 1) * WIDTH])
+
+        def quantise_weight(label, half):
+            codes, scales = weights[label]
+            cols = slice(half * PAIR * P, (half + 1) * PAIR * P)
+            nc.vector.quantize_mx(
+                out=codes[:, cols].bitcast(FP8X4),
+                scales=scales[:, cols],
+                in_=weight[label]["grouped"][:, half * WIDTH : (half + 1) * WIDTH],
+            )
 
         x_bank, x_grouped, x_codes, x_scales = {}, {}, {}, {}
         c_bank, sum_sq, rstd = {}, {}, {}
         h_rows, h_bank, h_grouped, h_codes, h_scales = {}, {}, {}, {}, {}
         kv_bank, kv_sb = {}, {}
-        weights = {}
 
         def in_range(i):
             return 0 <= i < N_PAIRS
@@ -138,8 +186,8 @@ def tile_deepseekv3attention_pb_t_kernel(
             nc.vector.quantize_mx(out=codes[:].bitcast(FP8X4), scales=scales[:], in_=grouped[:])
             return codes, scales
 
-        def multiply(out, codes, scales, j, weight):
-            w_codes, w_scales = weights[weight]
+        def multiply(out, codes, scales, j, label):
+            w_codes, w_scales = weights[label]
             cols = slice(j * P, (j + 1) * P)
             nc.tensor.matmul_mx(
                 out=out[:],
@@ -158,10 +206,9 @@ def tile_deepseekv3attention_pb_t_kernel(
                 at = first % LOAD_TILES
                 x_bank[i] = to_partitions(x_chunk[:, at : at + PAIR, :], psum_words, "words")
 
-        def regroup_x(i):
+        def regroup_x(i, copy):
             if in_range(i):
                 x_grouped[i] = scratch.tile([P, PAIR * P * 4], BF16, name="x_grouped", align_bytes=64)
-                copy = nc.vector.tensor_copy if i % 2 == 1 else nc.scalar.copy
                 regroup(copy, x_bank[i], x_grouped[i][:])
 
         def quantise_x(i):
@@ -216,28 +263,28 @@ def tile_deepseekv3attention_pb_t_kernel(
             if in_range(i):
                 h_bank[i] = to_partitions(h_rows[i][:], psum_words, "words")
 
-        def regroup_h(i):
+        def regroup_h(i, copy):
             if in_range(i):
                 h_grouped[i] = work.tile([P, PAIR * P * 4], BF16, name="h_grouped", align_bytes=64)
-                regroup(nc.vector.tensor_copy, h_bank[i], h_grouped[i][:])
+                regroup(copy, h_bank[i], h_grouped[i][:])
 
         def quantise_h(i):
             if in_range(i):
                 h_codes[i], h_scales[i] = quantise(work, h_grouped[i], "h")
 
-        def second_matmul(i):
+        def second_matmul(i, pool=psum_kv, name="kv_ps"):
             if in_range(i):
                 kv_bank[i] = []
                 for j in range(PAIR):
-                    kv_ps = psum_kv.tile([P, N_OUT], F32, name="kv_ps")
+                    kv_ps = pool.tile([P, N_OUT], F32, name=name)
                     multiply(kv_ps, h_codes[i], h_scales[i], j, "b")
                     kv_bank[i].append(kv_ps)
 
-        def copy_out(i, j):
+        def copy_out(i, j, copy):
             if in_range(i):
-                if j == 0:
+                if i not in kv_sb:
                     kv_sb[i] = results.tile([P, 2, PAIR, HEADS * HALF], F32, name="kv_sb")
-                nc.scalar.copy(
+                copy(
                     out=kv_sb[i][:, :, j, :].rearrange("p a (h d) -> p a h d", d=HALF),
                     in_=kv_bank[i][j][:].rearrange("p (h a d) -> p a h d", a=2, d=HALF),
                 )
@@ -248,31 +295,109 @@ def tile_deepseekv3attention_pb_t_kernel(
                 nc.sync.dma_start(out=k_rows[:, tiles, :], in_=kv_sb[i][:, 0, :, :])
                 nc.sync.dma_start(out=v_rows[:, tiles, :], in_=kv_sb[i][:, 1, :, :])
 
+        def store_tile(i, j):
+            tile = i * PAIR + j
+            nc.sync.dma_start(out=k_rows[:, tile : tile + 1, :], in_=kv_sb[i][:, 0, j : j + 1, :])
+            nc.sync.dma_start(out=v_rows[:, tile : tile + 1, :], in_=kv_sb[i][:, 1, j : j + 1, :])
+
+        on_vector = nc.vector.tensor_copy
+        on_scalar = nc.scalar.copy
+
+        RXM, RXV = 2, 1
+        XL = 3
+
         def step(n):
             quantise_x(n + 2)
             normalise(n)
             first_matmul(n + 2)
             quantise_h(n - 2)
             second_matmul(n - 2)
-            regroup_h(n - 1)
+            regroup_h(n - 1, on_vector)
             transpose_h(n)
-            regroup_x(n + 4)
-            transpose_x(n + 5)
+            regroup_x(n + XL, on_vector if n % RXM < RXV else on_scalar)
+            transpose_x(n + XL + 1)
             sum_squares(n + 2)
-            copy_out(n - 2, 0)
+            copy_out(n - 2, 0, on_scalar)
             root(n + 2)
-            copy_out(n - 2, 1)
+            copy_out(n - 2, 1, on_scalar)
             store(n - 2)
 
-        scaled_a = scale_weight(raw_a, factors_a, "a")
-        scaled_b = scale_weight(raw_b, factors_b, "b")
-        step(-5)
-        step(-4)
-        grouped_a = regroup_weight(nc.vector.tensor_copy, scaled_a, "a")
-        weights["a"] = quantise_weight(grouped_a, "a")
-        grouped_b = regroup_weight(nc.scalar.copy, scaled_b, "b")
-        step(-3)
-        step(-2)
-        weights["b"] = quantise_weight(grouped_b, "b")
-        for n in range(-1, N_PAIRS + 2):
+        new_weight("a", raw_a, factors_a)
+        new_weight("b", raw_b, factors_b)
+        scale_weight("a", 0)
+        scale_weight("a", 1)
+        transpose_weight("a", 0)
+        transpose_weight("a", 1)
+        regroup_weight(on_scalar, "a", 0)
+        regroup_weight(on_scalar, "a", 1)
+        transpose_x(0)
+        transpose_x(1)
+        quantise_weight("a", 0)
+        regroup_x(0, on_scalar)
+        quantise_weight("a", 1)
+        regroup_x(1, on_scalar)
+        quantise_x(0)
+        first_matmul(0)
+        scale_weight("b", 0)
+        transpose_x(2)
+        quantise_x(1)
+        first_matmul(1)
+        scale_weight("b", 1)
+        transpose_weight("b", 0)
+        transpose_weight("b", 1)
+        transpose_x(3)
+        sum_squares(0)
+        root(0)
+        regroup_x(2, on_vector)
+        sum_squares(1)
+        root(1)
+        normalise(0)
+        quantise_x(2)
+        first_matmul(2)
+        transpose_h(0)
+        regroup_x(3, on_scalar)
+        transpose_x(4)
+        regroup_weight(on_scalar, "b", 0)
+        sum_squares(2)
+        root(2)
+        normalise(1)
+        quantise_x(3)
+        first_matmul(3)
+        regroup_weight(on_scalar, "b", 1)
+        quantise_weight("b", 0)
+        regroup_h(0, on_vector)
+        transpose_h(1)
+        regroup_x(4, on_scalar)
+        transpose_x(5)
+        quantise_weight("b", 1)
+        sum_squares(3)
+        root(3)
+        LAST = N_PAIRS - 1
+        for n in range(2, N_PAIRS - 2):
             step(n)
+        quantise_h(LAST - 3)
+        second_matmul(LAST - 3)
+        regroup_h(LAST - 2, on_scalar)
+        normalise(LAST - 1)
+        transpose_h(LAST - 1)
+        normalise(LAST)
+        transpose_h(LAST)
+        copy_out(LAST - 3, 0, on_scalar)
+        copy_out(LAST - 3, 1, on_scalar)
+        store(LAST - 3)
+        regroup_h(LAST - 1, on_vector)
+        quantise_h(LAST - 2)
+        second_matmul(LAST - 2, psum_c, "c_ps")
+        quantise_h(LAST - 1)
+        second_matmul(LAST - 1)
+        regroup_h(LAST, on_vector)
+        copy_out(LAST - 2, 0, on_scalar)
+        store_tile(LAST - 2, 0)
+        copy_out(LAST - 2, 1, on_vector)
+        store_tile(LAST - 2, 1)
+        quantise_h(LAST)
+        second_matmul(LAST, psum_c, "c_ps")
+        for i in (LAST - 1, LAST):
+            for j in range(PAIR):
+                copy_out(i, j, on_scalar)
+                store_tile(i, j)

@@ -48,7 +48,6 @@ def tile_deepseekv3attention_pb_t_kernel(
         psum_words = ctx.enter_context(tc.psum_pool(name="psum_words", bufs=2))
         psum_c = ctx.enter_context(tc.psum_pool(name="psum_c", bufs=2 * PAIR))
         psum_kv = ctx.enter_context(tc.psum_pool(name="psum_kv", bufs=PAIR))
-        ctx.enter_context(tc.manual_schedule())
 
         HALVES = N_OUT // P // PAIR
 
@@ -223,17 +222,21 @@ def tile_deepseekv3attention_pb_t_kernel(
                     multiply(c_ps, x_codes[i], x_scales[i], j, "a")
                     c_bank[i].append(c_ps)
 
-        def sum_squares(i):
+        def square(i, j):
             if in_range(i):
-                sum_sq[i] = stats.tile([P, PAIR], F32, name="sum_sq")
-                for j in range(PAIR):
-                    squares = scratch.tile([P, N_OUT], BF16, name="squares")
-                    nc.scalar.activation(
-                        out=squares[:],
-                        in_=c_bank[i][j][:],
-                        func=ACT.Square,
-                        accum_out=sum_sq[i][:, j : j + 1],
-                    )
+                if i not in sum_sq:
+                    sum_sq[i] = stats.tile([P, PAIR], F32, name="sum_sq")
+                squares = scratch.tile([P, N_OUT], BF16, name="squares")
+                nc.scalar.activation(
+                    out=squares[:],
+                    in_=c_bank[i][j][:],
+                    func=ACT.Square,
+                    accum_out=sum_sq[i][:, j : j + 1],
+                )
+
+        def sum_squares(i):
+            for j in range(PAIR):
+                square(i, j)
 
         def root(i):
             if in_range(i):
@@ -304,7 +307,7 @@ def tile_deepseekv3attention_pb_t_kernel(
         on_scalar = nc.scalar.copy
 
         RXM, RXV = 2, 1
-        XL = 3
+        XL = 4
 
         def step(n):
             quantise_x(n + 2)
@@ -341,40 +344,45 @@ def tile_deepseekv3attention_pb_t_kernel(
         scale_weight("b", 0)
         transpose_x(2)
         quantise_x(1)
+        transpose_weight("b", 0)
         first_matmul(1)
         scale_weight("b", 1)
-        transpose_weight("b", 0)
         transpose_weight("b", 1)
         transpose_x(3)
-        sum_squares(0)
-        root(0)
         regroup_x(2, on_vector)
-        sum_squares(1)
-        root(1)
-        normalise(0)
-        quantise_x(2)
-        first_matmul(2)
-        transpose_h(0)
-        regroup_x(3, on_scalar)
         transpose_x(4)
-        regroup_weight(on_scalar, "b", 0)
-        sum_squares(2)
-        root(2)
+        regroup_weight(on_vector, "b", 0)
+        square(0, 0)
+        square(0, 1)
+        square(1, 0)
+        root(0)
+        square(1, 1)
+        quantise_x(2)
+        normalise(0)
+        first_matmul(2)
+        regroup_x(3, on_scalar)
+        root(1)
+        transpose_h(0)
         normalise(1)
+        sum_squares(2)
         quantise_x(3)
         first_matmul(3)
-        regroup_weight(on_scalar, "b", 1)
-        quantise_weight("b", 0)
+        regroup_x(4, on_scalar)
+        root(2)
+        transpose_x(5)
         regroup_h(0, on_vector)
         transpose_h(1)
-        regroup_x(4, on_scalar)
-        transpose_x(5)
+        regroup_weight(on_vector, "b", 1)
+        quantise_weight("b", 0)
         quantise_weight("b", 1)
         sum_squares(3)
+        regroup_x(5, on_scalar)
         root(3)
+        transpose_x(6)
         LAST = N_PAIRS - 1
-        for n in range(2, N_PAIRS - 2):
-            step(n)
+        with tc.manual_schedule():
+            for n in range(2, N_PAIRS - 2):
+                step(n)
         quantise_h(LAST - 3)
         second_matmul(LAST - 3)
         regroup_h(LAST - 2, on_scalar)

@@ -59,9 +59,9 @@ def tile_deepseekv3attention_pb_t_kernel(
             blocks = slice(half * PAIR, (half + 1) * PAIR)
             nc.sync.dma_start(out=raw[:, blocks, :], in_=rows[:, blocks, :])
 
-        def load_factors(s, label):
+        def load_factors(s, label, queue=nc.scalar):
             factors = keep.tile([P, (N_OUT // BLK) * (K // BLK)], BF16, name="factors_" + label)
-            nc.scalar.dma_start(
+            queue.dma_start(
                 out=factors[:], in_=s.rearrange("a b -> (a b)").partition_broadcast(P)
             )
             return factors
@@ -91,12 +91,12 @@ def tile_deepseekv3attention_pb_t_kernel(
         load_weight(raw_a, wkv_a_lat, 0)
         load_weight(raw_a, wkv_a_lat, 1)
         load_x(0, 2)
-        factors_b = load_factors(skv_b, "b")
+        factors_b = load_factors(skv_b, "b", nc.sync)
         load_weight(raw_b, wkv_b, 0)
         load_weight(raw_b, wkv_b, 1)
-        gain = keep.tile([P, K], BF16, name="gain")
-        nc.scalar.dma_start(out=gain[:], in_=kv_ln_w.partition_broadcast(P))
         load_x(1, 2)
+        gain = keep.tile([P, K], BF16, name="gain")
+        nc.sync.dma_start(out=gain[:], in_=kv_ln_w.partition_broadcast(P))
         for chunk in range(2, TILES // LOAD_TILES):
             load_x(chunk, 1)
 

@@ -380,9 +380,8 @@ def tile_deepseekv3attention_pb_t_kernel(
         root(3)
         transpose_x(6)
         LAST = N_PAIRS - 1
-        with tc.manual_schedule():
-            for n in range(2, N_PAIRS - 2):
-                step(n)
+        for n in range(2, N_PAIRS - 2):
+            step(n)
         quantise_h(LAST - 3)
         second_matmul(LAST - 3)
         regroup_h(LAST - 2, on_scalar)
@@ -393,7 +392,7 @@ def tile_deepseekv3attention_pb_t_kernel(
         copy_out(LAST - 3, 0, on_scalar)
         copy_out(LAST - 3, 1, on_scalar)
         store(LAST - 3)
-        regroup_h(LAST - 1, on_vector)
+        regroup_h(LAST - 1, on_scalar)
         quantise_h(LAST - 2)
         second_matmul(LAST - 2, psum_c, "c_ps")
         quantise_h(LAST - 1)
@@ -401,11 +400,12 @@ def tile_deepseekv3attention_pb_t_kernel(
         regroup_h(LAST, on_vector)
         copy_out(LAST - 2, 0, on_scalar)
         store_tile(LAST - 2, 0)
-        copy_out(LAST - 2, 1, on_vector)
+        copy_out(LAST - 2, 1, on_scalar)
         store_tile(LAST - 2, 1)
         quantise_h(LAST)
         second_matmul(LAST, psum_c, "c_ps")
         for i in (LAST - 1, LAST):
-            for j in range(PAIR):
-                copy_out(i, j, on_scalar)
-                store_tile(i, j)
+            copy_out(i, 0, on_scalar)
+            store_tile(i, 0)
+            copy_out(i, 1, on_vector)
+            store_tile(i, 1)

@@ -141,16 +141,17 @@ def tile_deepseekv3attention_pb_t_kernel(
 
         def scale_weight(label, half):
             w = weight[label]
-            blocks = PAIR * (K // BLK)
-            rows = slice(half * PAIR, (half + 1) * PAIR)
-            nc.vector.tensor_tensor(
-                out=w["scaled"][:, rows, :].rearrange("p b (i c) -> p (b i) c", c=BLK),
-                in0=w["raw"][:, rows, :].rearrange("p b (i c) -> p (b i) c", c=BLK),
-                in1=w["factors"][:, half * blocks : (half + 1) * blocks]
-                .unsqueeze(2)
-                .to_broadcast([P, blocks, BLK]),
-                op=ALU.mult,
-            )
+            for b in range(half * PAIR, (half + 1) * PAIR):
+                for i in range(K // BLK):
+                    cols = slice(i * BLK, (i + 1) * BLK)
+                    at = b * (K // BLK) + i
+                    nc.vector.tensor_scalar(
+                        out=w["scaled"][:, b, cols],
+                        in0=w["raw"][:, b, cols],
+                        scalar1=w["factors"][:, at : at + 1],
+                        scalar2=None,
+                        op0=ALU.mult,
+                    )
 
         def transpose_weight(label, half):
             w = weight[label]

from contextlib import ExitStack

import concourse.mybir as mybir
from concourse.masks import make_identity

BF16 = mybir.dt.bfloat16
F32 = mybir.dt.float32
U32 = mybir.dt.uint32
U8 = mybir.dt.uint8
FP8X4 = mybir.dt.float8_e4m3fn_x4
ACT = mybir.ActivationFunctionType
ALU = mybir.AluOpType

P = 128
S = 8192
K = 512
N_OUT = 512
BLK = 128
HEADS = 4
HALF = 64
EPS = 1e-6

WORDS = K // 2
TILES = S // P
PAIR = 2
N_PAIRS = TILES // PAIR
LOAD_TILES = 4

FLOPS = 2 * 2 * S * K * N_OUT


def tile_deepseekv3attention_pb_t_kernel(
    tc, hidden_states, wkv_a_lat, skv_a_lat, wkv_b, skv_b, kv_ln_w, out_0, out_1
):
    nc = tc.nc

    x_rows = hidden_states.rearrange("(p t) k -> p t k", t=TILES)
    k_rows = out_0.rearrange("(p t) h d -> p t (h d)", t=TILES)
    v_rows = out_1.rearrange("(p t) h d -> p t (h d)", t=TILES)

    with ExitStack() as ctx:
        keep = ctx.enter_context(tc.tile_pool(name="keep", bufs=1))
        work = ctx.enter_context(tc.tile_pool(name="work", bufs=2))
        ahead = ctx.enter_context(tc.tile_pool(name="ahead", bufs=8))
        stats = ctx.enter_context(tc.tile_pool(name="stats", bufs=3))
        scratch = ctx.enter_context(tc.tile_pool(name="scratch", bufs=4))
        results = ctx.enter_context(tc.tile_pool(name="results", bufs=8))
        psum_words = ctx.enter_context(tc.psum_pool(name="psum_words", bufs=2))
        psum_c = ctx.enter_context(tc.psum_pool(name="psum_c", bufs=2 * PAIR))
        psum_kv = ctx.enter_context(tc.psum_pool(name="psum_kv", bufs=PAIR))

        HALVES = N_OUT // P // PAIR

        def new_raw(label):
            return keep.tile([P, N_OUT // P, K], BF16, name="raw_" + label)

        def load_weight(raw, w, half):
            rows = w.rearrange("(b p) k -> p b k", p=P)
            blocks = slice(half * PAIR, (half + 1) * PAIR)
            nc.sync.dma_start(out=raw[:, blocks, :], in_=rows[:, blocks, :])

        def load_factors(s, label, queue=nc.scalar):
            factors = keep.tile([P, (N_OUT // BLK) * (K // BLK)], BF16, name="factors_" + label)
            queue.dma_start(
                out=factors[:], in_=s.rearrange("a b -> (a b)").partition_broadcast(P)
            )
            return factors

        x_sb = []

        def load_x(chunk, pieces):
            x_chunk = keep.tile([P, LOAD_TILES, K], BF16, name="x%d" % chunk)
            x_sb.append(x_chunk)
            for piece in range(pieces):
                load_piece(chunk, pieces, piece)

        def new_x(chunk):
            x_sb.append(keep.tile([P, LOAD_TILES, K], BF16, name="x%d" % chunk))

        def load_piece(chunk, pieces, piece):
            width = LOAD_TILES // pieces
            at = piece * width
            first = chunk * LOAD_TILES + at
            nc.sync.dma_start(
                out=x_sb[chunk][:, at : at + width, :], in_=x_rows[:, first : first + width, :]
            )

        factors_a = load_factors(skv_a_lat, "a")
        raw_a = new_raw("a")
        raw_b = new_raw("b")
        load_weight(raw_a, wkv_a_lat, 0)
        load_weight(raw_a, wkv_a_lat, 1)
        load_x(0, 2)
        factors_b = load_factors(skv_b, "b", nc.sync)
        load_weight(raw_b, wkv_b, 0)
        load_weight(raw_b, wkv_b, 1)
        load_x(1, 2)
        gain = keep.tile([P, K], BF16, name="gain")
        nc.sync.dma_start(out=gain[:], in_=kv_ln_w.partition_broadcast(P))
        for chunk in range(2, TILES // LOAD_TILES):
            load_x(chunk, 1)

        ident = keep.tile([P, P], F32, name="ident")
        make_identity(nc, ident[:])
        eps = keep.tile([P, 1], F32, name="eps")
        nc.vector.memset(eps[:], EPS)
        warm = keep.tile([P, 1], F32, name="warm")
        nc.scalar.activation(out=warm[:], in_=eps[:], func=ACT.Abs_reciprocal_sqrt)

        def to_partitions(rows, pool, name):
            bank = pool.tile([P, PAIR, 2, P], F32, name=name)
            words = rows.bitcast(F32)
            for j in range(PAIR):
                for u in range(2):
                    nc.tensor.transpose(
                        bank[:, j, u, :], words[:, j, u * P : (u + 1) * P], ident[:]
                    )
            return bank

        def regroup(copy, bank, grouped):
            copy(
                out=grouped.bitcast(F32).rearrange("p (j r u) -> p j r u", j=PAIR, u=2),
                in_=bank[:].rearrange("p j u r -> p j r u"),
            )

        WIDTH = PAIR * P * 4
        weight = {}
        weights = {}

        def new_weight(label, raw, factors):
            weight[label] = {
                "raw": raw,
                "factors": factors,
                "scaled": keep.tile([P, N_OUT // P, K], BF16, name="scaled_" + label),
                "grouped": keep.tile([P, N_OUT * 4], BF16, name="grouped_" + label, align_bytes=64),
                "bank": {},
            }
            codes = keep.tile([P, N_OUT], U32, name="codes_" + label, align_bytes=64)
            scales = keep.tile([P, N_OUT], U8, name="scales_" + label, align_bytes=64)
            weights[label] = (codes, scales)

        def scale_weight(label, half):
            w = weight[label]
            for b in range(half * PAIR, (half + 1) * PAIR):
                for i in range(K // BLK):
                    cols = slice(i * BLK, (i + 1) * BLK)
                    at = b * (K // BLK) + i
                    nc.vector.tensor_scalar(
                        out=w["scaled"][:, b, cols],
                        in0=w["raw"][:, b, cols],
                        scalar1=w["factors"][:, at : at + 1],
                        scalar2=None,
                        op0=ALU.mult,
                    )

        def transpose_weight(label, half):
            w = weight[label]
            w["bank"][half] = to_partitions(
                w["scaled"][:, half * PAIR : (half + 1) * PAIR, :], psum_kv, "kv_ps"
            )

        def regroup_weight(copy, label, half):
            w = weight[label]
            regroup(copy, w["bank"][half], w["grouped"][:, half * WIDTH : (half + 1) * WIDTH])

        def quantise_weight(label, half):
            codes, scales = weights[label]
            cols = slice(half * PAIR * P, (half + 1) * PAIR * P)
            nc.vector.quantize_mx(
                out=codes[:, cols].bitcast(FP8X4),
                scales=scales[:, cols],
                in_=weight[label]["grouped"][:, half * WIDTH : (half + 1) * WIDTH],
            )

        x_bank, x_grouped, x_codes, x_scales = {}, {}, {}, {}
        c_bank, sum_sq, rstd = {}, {}, {}
        h_rows, h_bank, h_grouped, h_codes, h_scales = {}, {}, {}, {}, {}
        kv_bank, kv_sb = {}, {}

        def in_range(i):
            return 0 <= i < N_PAIRS

        def quantise(pool, grouped, label):
            codes = pool.tile([P, PAIR * P], U32, name=label + "_codes", align_bytes=64)
            scales = pool.tile([P, PAIR * P], U8, name=label + "_scales", align_bytes=64)
            nc.vector.quantize_mx(out=codes[:].bitcast(FP8X4), scales=scales[:], in_=grouped[:])
            return codes, scales

        def multiply(out, codes, scales, j, label):
            w_codes, w_scales = weights[label]
            cols = slice(j * P, (j + 1) * P)
            nc.tensor.matmul_mx(
                out=out[:],
                lhsT=codes[:, cols].bitcast(FP8X4),
                lhsT_scale=scales[:, cols],
                rhs=w_codes[:].bitcast(FP8X4),
                rhs_scale=w_scales[:],
                start=True,
                stop=True,
            )

        def transpose_x(i):
            if in_range(i):
                first = i * PAIR
                x_chunk = x_sb[first // LOAD_TILES]
                at = first % LOAD_TILES
                x_bank[i] = to_partitions(x_chunk[:, at : at + PAIR, :], psum_words, "words")

        def regroup_x(i, copy):
            if in_range(i):
                x_grouped[i] = scratch.tile([P, PAIR * P * 4], BF16, name="x_grouped", align_bytes=64)
                regroup(copy, x_bank[i], x_grouped[i][:])

        def quantise_x(i):
            if in_range(i):
                x_codes[i], x_scales[i] = quantise(ahead, x_grouped[i], "x")

        def first_matmul(i):
            if in_range(i):
                c_bank[i] = []
                for j in range(PAIR):
                    c_ps = psum_c.tile([P, N_OUT], F32, name="c_ps")
                    multiply(c_ps, x_codes[i], x_scales[i], j, "a")
                    c_bank[i].append(c_ps)

        def square(i, j):
            if in_range(i):
                if i not in sum_sq:
                    sum_sq[i] = stats.tile([P, PAIR], F32, name="sum_sq")
                squares = scratch.tile([P, N_OUT], BF16, name="squares")
                nc.scalar.activation(
                    out=squares[:],
                    in_=c_bank[i][j][:],
                    func=ACT.Square,
                    accum_out=sum_sq[i][:, j : j + 1],
                )

        def sum_squares(i):
            for j in range(PAIR):
                square(i, j)

        def root(i):
            if in_range(i):
                rstd[i] = stats.tile([P, PAIR], F32, name="rstd")
                nc.scalar.activation(
                    out=rstd[i][:],
                    in_=sum_sq[i][:],
                    func=ACT.Abs_reciprocal_sqrt,
                    bias=eps[:, 0:1],
                    scale=1.0 / K,
                )

        def normalise(i):
            if in_range(i):
                h_rows[i] = work.tile([P, PAIR, K], BF16, name="h_rows")
                for j in range(PAIR):
                    nc.vector.scalar_tensor_tensor(
                        out=h_rows[i][:, j, :],
                        in0=c_bank[i][j][:],
                        scalar=rstd[i][:, j : j + 1],
                        in1=gain[:],
                        op0=ALU.mult,
                        op1=ALU.mult,
                    )

        def transpose_h(i):
            if in_range(i):
                h_bank[i] = to_partitions(h_rows[i][:], psum_words, "words")

        def regroup_h(i, copy):
            if in_range(i):
                h_grouped[i] = work.tile([P, PAIR * P * 4], BF16, name="h_grouped", align_bytes=64)
                regroup(copy, h_bank[i], h_grouped[i][:])

        def quantise_h(i):
            if in_range(i):
                h_codes[i], h_scales[i] = quantise(work, h_grouped[i], "h")

        def second_matmul(i, pool=psum_kv, name="kv_ps"):
            if in_range(i):
                kv_bank[i] = []
                for j in range(PAIR):
                    kv_ps = pool.tile([P, N_OUT], F32, name=name)
                    multiply(kv_ps, h_codes[i], h_scales[i], j, "b")
                    kv_bank[i].append(kv_ps)

        def copy_out(i, j, copy):
            if in_range(i):
                if i not in kv_sb:
                    kv_sb[i] = results.tile([P, 2, PAIR, HEADS * HALF], F32, name="kv_sb")
                copy(
                    out=kv_sb[i][:, :, j, :].rearrange("p a (h d) -> p a h d", d=HALF),
                    in_=kv_bank[i][j][:].rearrange("p (h a d) -> p a h d", a=2, d=HALF),
                )

        def store(i):
            if in_range(i):
                tiles = slice(i * PAIR, (i + 1) * PAIR)
                nc.sync.dma_start(out=k_rows[:, tiles, :], in_=kv_sb[i][:, 0, :, :])
                nc.sync.dma_start(out=v_rows[:, tiles, :], in_=kv_sb[i][:, 1, :, :])

        def store_tile(i, j):
            tile = i * PAIR + j
            nc.sync.dma_start(out=k_rows[:, tile : tile + 1, :], in_=kv_sb[i][:, 0, j : j + 1, :])
            nc.sync.dma_start(out=v_rows[:, tile : tile + 1, :], in_=kv_sb[i][:, 1, j : j + 1, :])

        on_vector = nc.vector.tensor_copy
        on_scalar = nc.scalar.copy

        RXM, RXV = 2, 1
        XL = 4

        def step(n):
            quantise_x(n + 2)
            normalise(n)
            first_matmul(n + 2)
            quantise_h(n - 2)
            second_matmul(n - 2)
            regroup_h(n - 1, on_vector)
            transpose_h(n)
            regroup_x(n + XL, on_vector if n % RXM < RXV else on_scalar)
            transpose_x(n + XL + 1)
            sum_squares(n + 2)
            copy_out(n - 2, 0, on_scalar)
            root(n + 2)
            copy_out(n - 2, 1, on_scalar)
            store(n - 2)

        new_weight("a", raw_a, factors_a)
        new_weight("b", raw_b, factors_b)
        scale_weight("a", 0)
        scale_weight("a", 1)
        transpose_weight("a", 0)
        transpose_weight("a", 1)
        regroup_weight(on_scalar, "a", 0)
        regroup_weight(on_scalar, "a", 1)
        transpose_x(0)
        transpose_x(1)
        quantise_weight("a", 0)
        regroup_x(0, on_scalar)
        quantise_weight("a", 1)
        regroup_x(1, on_scalar)
        quantise_x(0)
        first_matmul(0)
        scale_weight("b", 0)
        transpose_x(2)
        quantise_x(1)
        transpose_weight("b", 0)
        first_matmul(1)
        scale_weight("b", 1)
        transpose_weight("b", 1)
        transpose_x(3)
        regroup_x(2, on_vector)
        transpose_x(4)
        regroup_weight(on_vector, "b", 0)
        square(0, 0)
        square(0, 1)
        square(1, 0)
        root(0)
        square(1, 1)
        quantise_x(2)
        normalise(0)
        first_matmul(2)
        regroup_x(3, on_scalar)
        root(1)
        transpose_h(0)
        normalise(1)
        sum_squares(2)
        quantise_x(3)
        first_matmul(3)
        regroup_x(4, on_scalar)
        root(2)
        transpose_x(5)
        regroup_h(0, on_vector)
        transpose_h(1)
        regroup_weight(on_vector, "b", 1)
        quantise_weight("b", 0)
        quantise_weight("b", 1)
        sum_squares(3)
        regroup_x(5, on_scalar)
        root(3)
        transpose_x(6)
        LAST = N_PAIRS - 1
        for n in range(2, N_PAIRS - 2):
            step(n)
        quantise_h(LAST - 3)
        second_matmul(LAST - 3)
        regroup_h(LAST - 2, on_scalar)
        normalise(LAST - 1)
        transpose_h(LAST - 1)
        normalise(LAST)
        transpose_h(LAST)
        copy_out(LAST - 3, 0, on_scalar)
        copy_out(LAST - 3, 1, on_scalar)
        store(LAST - 3)
        regroup_h(LAST - 1, on_scalar)
        quantise_h(LAST - 2)
        second_matmul(LAST - 2, psum_c, "c_ps")
        quantise_h(LAST - 1)
        second_matmul(LAST - 1)
        regroup_h(LAST, on_vector)
        copy_out(LAST - 2, 0, on_scalar)
        store_tile(LAST - 2, 0)
        copy_out(LAST - 2, 1, on_scalar)
        store_tile(LAST - 2, 1)
        quantise_h(LAST)
        second_matmul(LAST, psum_c, "c_ps")
        for i in (LAST - 1, LAST):
            copy_out(i, 0, on_scalar)
            store_tile(i, 0)
            copy_out(i, 1, on_vector)
            store_tile(i, 1)
